import numpy as np
import ml_dtypes


def mxq(x, axis, fmt="e4m3"):
    dtype, down = {"e4m3": (ml_dtypes.float8_e4m3fn, 7), "e5m2": (ml_dtypes.float8_e5m2, 14)}[fmt]
    v = np.moveaxis(np.asarray(x, np.float32).astype(ml_dtypes.bfloat16).astype(np.float64), axis, -1)
    blocks = v.reshape(v.shape[:-1] + (-1, 32))
    amax = np.abs(blocks).max(-1, keepdims=True)
    byte = np.maximum(np.where(amax > 0, np.frexp(amax)[1] - 1 + 127, 0) - down, 1)
    scale = np.exp2(byte - 127.0)
    codes = (blocks / scale).astype(np.float32).astype(dtype).astype(np.float64)
    return np.moveaxis((codes * scale).reshape(v.shape), -1, axis)


WIDE = False


def mx_kscale(k):
    if not WIDE:
        return np.ones(k)
    levels = np.array([10, -10, 5, -5, 0])
    if k % 512:
        return np.exp2(np.random.permutation(np.resize(levels, k // 32))).repeat(32)
    a = np.empty((k // 512, 16))
    for p in range(k // 512):
        a[p, :8] = np.random.permutation(np.resize(levels, 8))
        for g in range(8):
            far = levels[np.abs(levels - a[p, g]) >= 10]
            a[p, g + 8] = far[np.random.randint(len(far))]
    return np.exp2(a.ravel()).repeat(32)


BF16 = ml_dtypes.bfloat16


def bf(x):
    return np.asarray(x, np.float32).astype(BF16)


def f64(x):
    return np.asarray(x).astype(np.float64)


B, T, C, N_HEAD, N_KV, D_LAT, D_ROPE = 2, 2048, 1024, 8, 4, 512, 64
HD = C // N_HEAD
D_NOPE = HD - D_ROPE
DR2 = D_ROPE // 2
ROPE_BASE = 10000.0
EPS = 1.1920928955078125e-07


def rope_tables():
    half = HD // 2
    inv_freq = 1.0 / (ROPE_BASE ** (np.arange(half) / half))
    ang = np.arange(T)[:, None] * inv_freq[None, :DR2]
    return np.cos(ang), np.sin(ang)


def rms(u):
    return u * (1.0 / np.sqrt(np.mean(u * u, axis=-1, keepdims=True) + EPS))


def draw0():
    s, t = mx_kscale(C), mx_kscale(D_LAT)
    cos, sin = rope_tables()
    return {"x": bf(np.random.standard_normal((B, T, C)) * s),
            "cos": bf(cos), "sin": bf(sin),
            "w_kv": bf(np.random.standard_normal((C, D_LAT)) / np.sqrt(C) / s[:, None] * t),
            "w_kup": bf(np.random.standard_normal((D_LAT, N_KV * D_NOPE)) / np.sqrt(D_LAT) / t[:, None]),
            "w_vup": bf(np.random.standard_normal((D_LAT, N_KV * HD)) / np.sqrt(D_LAT) / t[:, None]),
            "w_krope": bf(np.random.standard_normal((C, N_KV * D_ROPE)) / np.sqrt(C) / s[:, None])}


def core(x, cos, sin, w_kv, w_kup, w_vup, w_krope):
    xq = mxq(f64(x), 2, "e4m3")
    latent = xq @ mxq(f64(w_kv), 0, "e4m3")
    lq = mxq(latent, 2, "e4m3")
    k_nope = (lq @ mxq(f64(w_kup), 0, "e4m3")).reshape(B, T, N_KV, D_NOPE)
    r = (xq @ mxq(f64(w_krope), 0, "e4m3")).reshape(B, T, N_KV, D_ROPE)
    c, sn = f64(cos)[None, :, None, :], f64(sin)[None, :, None, :]
    r1, r2 = r[..., :DR2], r[..., DR2:]
    k_rope = np.concatenate([r1 * c + r2 * sn, -r1 * sn + r2 * c], axis=-1)
    k = rms(np.concatenate([k_rope, k_nope], axis=-1))
    v = (lq @ mxq(f64(w_vup), 0, "e4m3")).reshape(B, T, N_KV, HD)
    return k, v


def e4m3fn_bytes(y):
    return np.clip(np.asarray(y, np.float64), -448.0, 448.0).astype(np.float32).astype(ml_dtypes.float8_e4m3fn).view(np.uint8)


def e4m3fn_values(b):
    return np.asarray(b, np.uint8).view(ml_dtypes.float8_e4m3fn).astype(np.float64)


def setup_inputs():
    d = draw0()
    x0 = np.asarray(d['x']).astype(np.float64)
    s = (np.max(np.abs(x0), axis=(0, 1), keepdims=True) / 448.0).astype(np.float32)
    out = {}
    for k, v in d.items():
        if k == 'x':
            out['x_bytes'] = e4m3fn_bytes(x0 / s.astype(np.float64))
            out['x_scale'] = s
        else:
            out[k] = v
    return out


def reference(x_bytes, x_scale, cos, sin, w_kv, w_kup, w_vup, w_krope):
    return core(e4m3fn_values(x_bytes) * x_scale.astype(np.float64), cos, sin, w_kv, w_kup, w_vup, w_krope)

@@ -1,0 +1,233 @@
+from contextlib import ExitStack
+
+import concourse.mybir as mybir
+from concourse.masks import make_identity
+
+F32 = mybir.dt.float32
+BF16 = mybir.dt.bfloat16
+U32 = mybir.dt.uint32
+U8 = mybir.dt.uint8
+FP8 = mybir.dt.float8_e4m3fn
+FP8X4 = mybir.dt.float8_e4m3fn_x4
+ADD = mybir.AluOpType.add
+MULT = mybir.AluOpType.mult
+ACT = mybir.ActivationFunctionType
+
+P = 128
+B, T, C = 2, 2048, 1024
+D_LAT = 512
+H, HD, D_ROPE = 4, 128, 64
+R2 = D_ROPE // 2
+PASSES = C // 512
+TILES = T // P
+PAIRS = B * TILES // 2
+EPS = 1.1920928955078125e-07
+
+FLOPS = 2 * B * T * (C * D_LAT + D_LAT * H * (HD - D_ROPE) + D_LAT * H * HD + C * H * D_ROPE)
+
+
+def tile_mlacausalselfattention_pa_t_kernel(tc, x_bytes, x_scale, cos, sin, w_kv, w_kup, w_vup, w_krope, out_0, out_1):
+    nc = tc.nc
+    with ExitStack() as ctx:
+        keep = ctx.enter_context(tc.tile_pool(name="keep", bufs=1))
+        stage = ctx.enter_context(tc.tile_pool(name="stage", bufs=1))
+        work = ctx.enter_context(tc.tile_pool(name="work", bufs=3))
+        psum = ctx.enter_context(tc.psum_pool(name="psum", bufs=1))
+
+        x_view = x_bytes.rearrange("b (p i) k -> b p (i k)", p=P)
+        xt = []
+        for j in range(PAIRS):
+            xt.append(keep.tile([P, 2 * C], U8, name="xbytes%d" % j))
+
+        def load_x(j):
+            b, i = divmod(2 * j, TILES)
+            nc.sync.dma_start(out=xt[j][:], in_=x_view[b][:, i * C:(i + 2) * C])
+
+        load_x(0)
+        sc = keep.tile([P, PASSES, 4], F32, name="sc")
+        nc.scalar.dma_start(out=sc[:], in_=x_scale.rearrange("a b k -> (a b k)").rearrange("(g p t) -> p g t", p=P, t=4))
+        raw_kv = []
+        for g in range(PASSES):
+            t = stage.tile([P, 4, D_LAT], BF16, name="raw_kv%d" % g)
+            nc.sync.dma_start(out=t[:], in_=w_kv.rearrange("(g p j) c -> g p j c", p=P, j=4)[g])
+            raw_kv.append(t)
+        raw_kr = []
+        for g in range(PASSES):
+            t = stage.tile([P, 4, H * D_ROPE], BF16, name="raw_kr%d" % g)
+            nc.sync.dma_start(out=t[:], in_=w_krope.rearrange("(g p j) c -> g p j c", p=P, j=4)[g])
+            raw_kr.append(t)
+        load_x(1)
+        raw_ku = stage.tile([P, 4, 256], BF16, name="raw_ku")
+        nc.sync.dma_start(out=raw_ku[:], in_=w_kup.rearrange("(p j) c -> p j c", j=4))
+        raw_vu = stage.tile([P, 4, 512], BF16, name="raw_vu")
+        nc.sync.dma_start(out=raw_vu[:], in_=w_vup.rearrange("(p j) c -> p j c", j=4))
+        cs = stage.tile([P, TILES, R2], BF16, name="cs")
+        nc.sync.dma_start(out=cs[:], in_=cos.rearrange("(p i) q -> p i q", p=P))
+        sn = stage.tile([P, TILES, R2], BF16, name="sn")
+        nc.sync.dma_start(out=sn[:], in_=sin.rearrange("(p i) q -> p i q", p=P))
+        for j in range(2, PAIRS):
+            load_x(j)
+
+        ident = keep.tile([P, P], F32, name="ident")
+        make_identity(nc, ident[:])
+
+        wkv_q = keep.tile([P, PASSES, D_LAT], U32, name="wkv_q", align_bytes=64)
+        wkv_s = keep.tile([P, PASSES, D_LAT], U8, name="wkv_s", align_bytes=64)
+        wkr_q = keep.tile([P, PASSES, 256], U32, name="wkr_q", align_bytes=64)
+        wkr_s = keep.tile([P, PASSES, 256], U8, name="wkr_s", align_bytes=64)
+        wku_q = keep.tile([P, 256], U32, name="wku_q", align_bytes=64)
+        wku_s = keep.tile([P, 256], U8, name="wku_s", align_bytes=64)
+        wvu_q = keep.tile([P, 512], U32, name="wvu_q", align_bytes=64)
+        wvu_s = keep.tile([P, 512], U8, name="wvu_s", align_bytes=64)
+
+        def quant(codes, scales, src):
+            nc.vector.quantize_mx(out=codes.bitcast(FP8X4), scales=scales, in_=src)
+
+        kv_il = []
+        for g in range(PASSES):
+            t = stage.tile([P, 4 * D_LAT], BF16, name="kv_il%d" % g, align_bytes=64)
+            dst = t[:].rearrange("p (t m j) -> p t m j", t=4, j=4)
+            src = raw_kv[g][:].rearrange("p j (m t) -> p t m j", t=4)
+            if g == 0:
+                nc.scalar.copy(out=dst, in_=src)
+            else:
+                nc.vector.tensor_copy(out=dst, in_=src)
+            kv_il.append(t)
+        for g in range(PASSES):
+            quant(wkv_q[:, g, :], wkv_s[:, g, :], kv_il[g][:])
+
+        def weight(raw, width, codes, scales, name, eng):
+            t = stage.tile([P, width * 4], BF16, name=name, align_bytes=64)
+            dst = t[:].rearrange("p (c j) -> p c j", j=4)
+            src = raw[:].rearrange("p j c -> p c j")
+            if eng == "s":
+                nc.scalar.copy(out=dst, in_=src)
+            else:
+                nc.vector.tensor_copy(out=dst, in_=src)
+            quant(codes, scales, t[:])
+
+        def cast(j):
+            xb = work.tile([P, 2, C], BF16, name="xb", bufs=4)
+            for s in range(2):
+                src = xt[j][:, s * C:(s + 1) * C].bitcast(FP8)
+                if j == 0 and s == 0:
+                    nc.vector.tensor_copy(out=xb[:, s, :], in_=src)
+                elif j == 0:
+                    nc.scalar.copy(out=xb[:, s, :], in_=src)
+                else:
+                    nc.gpsimd.tensor_copy(out=xb[:, s, :], in_=src)
+            return xb
+
+        def front(j, xb):
+            xg = work.tile([P, PASSES, 1024], BF16, name="xg", align_bytes=64)
+            xq = work.tile([P, PASSES, 256], U32, name="xq", align_bytes=64)
+            xs = work.tile([P, PASSES, 256], U8, name="xs", align_bytes=64)
+            for g in range(PASSES):
+                px = psum.tile([P, 2, 256], F32, name="px", bufs=2)
+                for s in range(2):
+                    words = xb[:, s, :].bitcast(F32)
+                    for u in range(2):
+                        nc.tensor.transpose(px[:, u, s * P:(s + 1) * P], words[:, 256 * g + u:256 * (g + 1):2], ident[:])
+                nc.vector.tensor_tensor(
+                    out=xg[:, g, :].rearrange("p (n u e) -> p n u e", u=2, e=2),
+                    in0=px[:].bitcast(BF16).rearrange("p u (n e) -> p n u e", e=2),
+                    in1=sc[:, g, :].rearrange("p (u e) -> p u e", e=2).unsqueeze(1).to_broadcast([P, 256, 2, 2]),
+                    op=MULT)
+            for g in range(PASSES):
+                quant(xq[:, g, :], xs[:, g, :], xg[:, g, :])
+            return xq, xs
+
+        def latent(j, xq, xs):
+            lg = work.tile([P, 2, 512], BF16, name="lg", align_bytes=64)
+            lq = work.tile([P, 256], U32, name="lq", align_bytes=64)
+            ls = work.tile([P, 256], U8, name="ls", align_bytes=64)
+            for s in range(2):
+                lat = psum.tile([P, 4, P], F32, name="lat", bufs=2)
+                for t in range(4):
+                    for g in range(PASSES):
+                        nc.tensor.matmul_mx(
+                            out=lat[:, t, :],
+                            lhsT=wkv_q[:, g, t * P:(t + 1) * P].bitcast(FP8X4), lhsT_scale=wkv_s[:, g, t * P:(t + 1) * P],
+                            rhs=xq[:, g, s * P:(s + 1) * P].bitcast(FP8X4), rhs_scale=xs[:, g, s * P:(s + 1) * P],
+                            start=(g == 0), stop=(g == PASSES - 1))
+                nc.scalar.copy(out=lg[:, s, :].rearrange("p (n t) -> p n t", t=4), in_=lat[:].rearrange("p t n -> p n t"))
+            quant(lq[:], ls[:], lg[:].rearrange("p s w -> p (s w)"))
+            return lq, ls
+
+        def back(j, xq, xs, lq, ls):
+            b, i = divmod(2 * j, TILES)
+            kc = work.tile([P, 2, H, HD], F32, name="kc")
+            vo = work.tile([P, 2, 512], F32, name="vo")
+            pr = psum.tile([P, 2, 256], F32, name="pr")
+            pn = psum.tile([P, 2, 256], F32, name="pn")
+            for s in range(2):
+                for g in range(PASSES):
+                    nc.tensor.matmul_mx(
+                        out=pr[:, s, :],
+                        lhsT=xq[:, g, s * P:(s + 1) * P].bitcast(FP8X4), lhsT_scale=xs[:, g, s * P:(s + 1) * P],
+                        rhs=wkr_q[:, g, :].bitcast(FP8X4), rhs_scale=wkr_s[:, g, :],
+                        start=(g == 0), stop=(g == PASSES - 1))
+            for s in range(2):
+                nc.tensor.matmul_mx(
+                    out=pn[:, s, :],
+                    lhsT=lq[:, s * P:(s + 1) * P].bitcast(FP8X4), lhsT_scale=ls[:, s * P:(s + 1) * P],
+                    rhs=wku_q[:].bitcast(FP8X4), rhs_scale=wku_s[:], start=True, stop=True)
+            pvs = []
+            for s in range(2):
+                pv = psum.tile([P, 512], F32, name="pv", bufs=2)
+                nc.tensor.matmul_mx(
+                    out=pv[:],
+                    lhsT=lq[:, s * P:(s + 1) * P].bitcast(FP8X4), lhsT_scale=ls[:, s * P:(s + 1) * P],
+                    rhs=wvu_q[:].bitcast(FP8X4), rhs_scale=wvu_s[:], start=True, stop=True)
+                pvs.append(pv)
+            prods = []
+            for tab in (tab_c, tab_s):
+                pd = work.tile([P, 2, H, D_ROPE], F32, name="pd", bufs=4)
+                nc.vector.tensor_tensor(
+                    out=pd[:], in0=pr[:].rearrange("p s (h d) -> p s h d", h=H),
+                    in1=tab[:, i:i + 2, :].unsqueeze(2).to_broadcast([P, 2, H, D_ROPE]), op=MULT)
+                prods.append(pd)
+            a = prods[0][:].rearrange("p s h (j q) -> p (s h) j q", j=2)
+            bb = prods[1][:].rearrange("p s h (j q) -> p (s h) j q", j=2)
+            kcv = kc[:].rearrange("p s h d -> p (s h) d")
+            nc.scalar.copy(out=kcv[:, :, D_ROPE:], in_=pn[:].rearrange("p s (h d) -> p (s h) d", h=H))
+            nc.vector.tensor_tensor(out=kcv[:, :, 0:D_ROPE].rearrange("p m (j q) -> p m j q", j=2), in0=a, in1=bb[:, :, ::-1, :], op=ADD)
+            ssq = work.tile([P, 2 * H], F32, name="ssq")
+            rinv = work.tile([P, 2 * H], F32, name="rinv")
+            for m in range(2 * H):
+                junk = work.tile([P, HD], F32, name="junk", bufs=2)
+                nc.scalar.activation(out=junk[:], in_=kcv[:, m, :], func=ACT.Square, accum_out=ssq[:, m:m + 1])
+            nc.scalar.activation(out=rinv[:], in_=ssq[:], func=ACT.Abs_reciprocal_sqrt, scale=1.0 / HD, bias=EPS)
+            ko = work.tile([P, 2, H, HD], F32, name="ko")
+            kov = ko[:].rearrange("p s h d -> p (s h) d")
+            for m in range(2 * H):
+                if m % 8 in (0, 3, 6):
+                    nc.scalar.activation(out=kov[:, m, :], in_=kcv[:, m, :], func=ACT.Copy, scale=rinv[:, m:m + 1])
+                else:
+                    nc.vector.tensor_scalar(out=kov[:, m, :], in0=kcv[:, m, :], scalar1=rinv[:, m:m + 1], scalar2=None, op0=MULT)
+            for s in range(2):
+                nc.scalar.copy(out=vo[:, s, :], in_=pvs[s][:])
+            nc.sync.dma_start(out=out_1.rearrange("b (p i) h d -> b p i (h d)", p=P)[b][:, i:i + 2, :], in_=vo[:])
+            nc.sync.dma_start(out=out_0.rearrange("b (p i) h d -> b p i (h d)", p=P)[b][:, i:i + 2, :], in_=ko[:].rearrange("p s h d -> p s (h d)"))
+
+        xb = {}
+        xq = {}
+        lq = {}
+        xb[0] = cast(0)
+        xq[0] = front(0, xb[0])
+        weight(raw_kr[0], 256, wkr_q[:, 0, :], wkr_s[:, 0, :], "kr_il0", "s")
+        weight(raw_kr[1], 256, wkr_q[:, 1, :], wkr_s[:, 1, :], "kr_il1", "v")
+        weight(raw_ku, 256, wku_q[:], wku_s[:], "ku_il", "s")
+        weight(raw_vu, 512, wvu_q[:], wvu_s[:], "vu_il", "v")
+        tab_c = keep.tile([P, TILES, D_ROPE], BF16, name="tab_c")
+        tab_s = keep.tile([P, TILES, D_ROPE], BF16, name="tab_s")
+        nc.vector.tensor_copy(out=tab_c[:, :, 0:R2], in_=cs[:])
+        nc.vector.tensor_copy(out=tab_c[:, :, R2:], in_=cs[:])
+        nc.vector.tensor_scalar(out=tab_s[:, :, 0:R2], in0=sn[:], scalar1=-1.0, scalar2=None, op0=MULT)
+        nc.vector.tensor_copy(out=tab_s[:, :, R2:], in_=sn[:])
+        for j in range(PAIRS):
+            lq[j] = latent(j, *xq[j])
+            if j + 1 < PAIRS:
+                xb[j + 1] = cast(j + 1)
+                xq[j + 1] = front(j + 1, xb[j + 1])
+            back(j, *xq[j], *lq[j])

@@ -70,6 +70,11 @@ def tile_mlacausalselfattention_pa_t_kernel(tc, x_bytes, x_scale, cos, sin, w_kv
 
         ident = keep.tile([P, P], F32, name="ident")
         make_identity(nc, ident[:])
+        warm = keep.tile([P, 1], F32, name="warm")
+        warm2 = keep.tile([P, 1], F32, name="warm2")
+        token = keep.tile([P, 1], F32, name="token")
+        nc.gpsimd.memset(warm[:], 1.0)
+        nc.scalar.activation(out=warm2[:], in_=warm[:], func=ACT.Abs_reciprocal_sqrt, scale=1.0 / HD, bias=EPS)
 
         wkv_q = keep.tile([P, PASSES, D_LAT], U32, name="wkv_q", align_bytes=64)
         wkv_s = keep.tile([P, PASSES, D_LAT], U8, name="wkv_s", align_bytes=64)
@@ -79,155 +84,208 @@ def tile_mlacausalselfattention_pa_t_kernel(tc, x_bytes, x_scale, cos, sin, w_kv
         wku_s = keep.tile([P, 256], U8, name="wku_s", align_bytes=64)
         wvu_q = keep.tile([P, 512], U32, name="wvu_q", align_bytes=64)
         wvu_s = keep.tile([P, 512], U8, name="wvu_s", align_bytes=64)
+        tab_c = keep.tile([P, TILES, D_ROPE], BF16, name="tab_c")
+        tab_s = keep.tile([P, TILES, D_ROPE], BF16, name="tab_s")
 
         def quant(codes, scales, src):
             nc.vector.quantize_mx(out=codes.bitcast(FP8X4), scales=scales, in_=src)
 
-        kv_il = []
-        for g in range(PASSES):
-            t = stage.tile([P, 4 * D_LAT], BF16, name="kv_il%d" % g, align_bytes=64)
-            dst = t[:].rearrange("p (t m j) -> p t m j", t=4, j=4)
-            src = raw_kv[g][:].rearrange("p j (m t) -> p t m j", t=4)
-            if g == 0:
-                nc.scalar.copy(out=dst, in_=src)
-            else:
-                nc.vector.tensor_copy(out=dst, in_=src)
-            kv_il.append(t)
-        for g in range(PASSES):
-            quant(wkv_q[:, g, :], wkv_s[:, g, :], kv_il[g][:])
-
-        def weight(raw, width, codes, scales, name, eng):
-            t = stage.tile([P, width * 4], BF16, name=name, align_bytes=64)
-            dst = t[:].rearrange("p (c j) -> p c j", j=4)
-            src = raw[:].rearrange("p j c -> p c j")
+        def copy(eng, dst, src):
             if eng == "s":
                 nc.scalar.copy(out=dst, in_=src)
-            else:
+            elif eng == "v":
                 nc.vector.tensor_copy(out=dst, in_=src)
-            quant(codes, scales, t[:])
+            else:
+                nc.gpsimd.tensor_copy(out=dst, in_=src)
 
-        def cast(j):
-            xb = work.tile([P, 2, C], BF16, name="xb", bufs=4)
+        def interleave_kv(g, eng):
+            t = stage.tile([P, 4 * D_LAT], BF16, name="kv_il%d" % g, align_bytes=64)
+            copy(eng, t[:].rearrange("p (t m j) -> p t m j", t=4, j=4), raw_kv[g][:].rearrange("p j (m t) -> p t m j", t=4))
+            return t
+
+        def interleave(raw, width, name, eng):
+            t = stage.tile([P, width * 4], BF16, name=name, align_bytes=64)
+            copy(eng, t[:].rearrange("p (c j) -> p c j", j=4), raw[:].rearrange("p j c -> p c j"))
+            return t
+
+        def cast(j, engs):
+            xb[j] = work.tile([P, 2, C], BF16, name="xb", bufs=3)
             for s in range(2):
-                src = xt[j][:, s * C:(s + 1) * C].bitcast(FP8)
-                if j == 0 and s == 0:
-                    nc.vector.tensor_copy(out=xb[:, s, :], in_=src)
-                elif j == 0:
-                    nc.scalar.copy(out=xb[:, s, :], in_=src)
-                else:
-                    nc.gpsimd.tensor_copy(out=xb[:, s, :], in_=src)
-            return xb
+                copy(engs[s], xb[j][:, s, :], xt[j][:, s * C:(s + 1) * C].bitcast(FP8))
 
-        def front(j, xb):
-            xg = work.tile([P, PASSES, 1024], BF16, name="xg", align_bytes=64)
-            xq = work.tile([P, PASSES, 256], U32, name="xq", align_bytes=64)
-            xs = work.tile([P, PASSES, 256], U8, name="xs", align_bytes=64)
+        def turn(j):
+            px[j] = []
             for g in range(PASSES):
-                px = psum.tile([P, 2, 256], F32, name="px", bufs=2)
+                bank = psum.tile([P, 2, 256], F32, name="px", bufs=2)
                 for s in range(2):
-                    words = xb[:, s, :].bitcast(F32)
+                    words = xb[j][:, s, :].bitcast(F32)
                     for u in range(2):
-                        nc.tensor.transpose(px[:, u, s * P:(s + 1) * P], words[:, 256 * g + u:256 * (g + 1):2], ident[:])
+                        nc.tensor.transpose(bank[:, u, s * P:(s + 1) * P], words[:, 256 * g + u:256 * (g + 1):2], ident[:])
+                px[j].append(bank)
+
+        def scale_x(j):
+            xg[j] = work.tile([P, PASSES, 1024], BF16, name="xg", align_bytes=64)
+            for g in range(PASSES):
                 nc.vector.tensor_tensor(
-                    out=xg[:, g, :].rearrange("p (n u e) -> p n u e", u=2, e=2),
-                    in0=px[:].bitcast(BF16).rearrange("p u (n e) -> p n u e", e=2),
+                    out=xg[j][:, g, :].rearrange("p (n u e) -> p n u e", u=2, e=2),
+                    in0=px[j][g][:].bitcast(BF16).rearrange("p u (n e) -> p n u e", e=2),
                     in1=sc[:, g, :].rearrange("p (u e) -> p u e", e=2).unsqueeze(1).to_broadcast([P, 256, 2, 2]),
                     op=MULT)
-            for g in range(PASSES):
-                quant(xq[:, g, :], xs[:, g, :], xg[:, g, :])
-            return xq, xs
 
-        def latent(j, xq, xs):
-            lg = work.tile([P, 2, 512], BF16, name="lg", align_bytes=64)
-            lq = work.tile([P, 256], U32, name="lq", align_bytes=64)
-            ls = work.tile([P, 256], U8, name="ls", align_bytes=64)
+        def quant_x(j):
+            xq[j] = work.tile([P, PASSES, 256], U32, name="xq", align_bytes=64)
+            xs[j] = work.tile([P, PASSES, 256], U8, name="xs", align_bytes=64)
+            for g in range(PASSES):
+                quant(xq[j][:, g, :], xs[j][:, g, :], xg[j][:, g, :])
+
+        def latent(j):
+            lat[j] = []
             for s in range(2):
-                lat = psum.tile([P, 4, P], F32, name="lat", bufs=2)
+                bank = psum.tile([P, 4, P], F32, name="lat", bufs=2)
                 for t in range(4):
                     for g in range(PASSES):
                         nc.tensor.matmul_mx(
-                            out=lat[:, t, :],
+                            out=bank[:, t, :],
                             lhsT=wkv_q[:, g, t * P:(t + 1) * P].bitcast(FP8X4), lhsT_scale=wkv_s[:, g, t * P:(t + 1) * P],
-                            rhs=xq[:, g, s * P:(s + 1) * P].bitcast(FP8X4), rhs_scale=xs[:, g, s * P:(s + 1) * P],
+                            rhs=xq[j][:, g, s * P:(s + 1) * P].bitcast(FP8X4), rhs_scale=xs[j][:, g, s * P:(s + 1) * P],
                             start=(g == 0), stop=(g == PASSES - 1))
-                nc.scalar.copy(out=lg[:, s, :].rearrange("p (n t) -> p n t", t=4), in_=lat[:].rearrange("p t n -> p n t"))
-            quant(lq[:], ls[:], lg[:].rearrange("p s w -> p (s w)"))
-            return lq, ls
+                lat[j].append(bank)
 
-        def back(j, xq, xs, lq, ls):
-            b, i = divmod(2 * j, TILES)
-            kc = work.tile([P, 2, H, HD], F32, name="kc")
-            vo = work.tile([P, 2, 512], F32, name="vo")
-            pr = psum.tile([P, 2, 256], F32, name="pr")
-            pn = psum.tile([P, 2, 256], F32, name="pn")
+        def empty_latent(j):
+            lg[j] = work.tile([P, 2, 512], BF16, name="lg", align_bytes=64)
+            for s in range(2):
+                nc.scalar.copy(out=lg[j][:, s, :].rearrange("p (n t) -> p n t", t=4), in_=lat[j][s][:].rearrange("p t n -> p n t"))
+
+        def quant_latent(j):
+            lq[j] = work.tile([P, 256], U32, name="lq", align_bytes=64)
+            ls[j] = work.tile([P, 256], U8, name="ls", align_bytes=64)
+            quant(lq[j][:], ls[j][:], lg[j][:].rearrange("p s w -> p (s w)"))
+
+        def rope_mm(j):
+            pr[j] = psum.tile([P, 2, 256], F32, name="pr")
             for s in range(2):
                 for g in range(PASSES):
                     nc.tensor.matmul_mx(
-                        out=pr[:, s, :],
-                        lhsT=xq[:, g, s * P:(s + 1) * P].bitcast(FP8X4), lhsT_scale=xs[:, g, s * P:(s + 1) * P],
+                        out=pr[j][:, s, :],
+                        lhsT=xq[j][:, g, s * P:(s + 1) * P].bitcast(FP8X4), lhsT_scale=xs[j][:, g, s * P:(s + 1) * P],
                         rhs=wkr_q[:, g, :].bitcast(FP8X4), rhs_scale=wkr_s[:, g, :],
                         start=(g == 0), stop=(g == PASSES - 1))
+
+        def up_mm(j):
+            pn[j] = psum.tile([P, 2, 256], F32, name="pn")
             for s in range(2):
                 nc.tensor.matmul_mx(
-                    out=pn[:, s, :],
-                    lhsT=lq[:, s * P:(s + 1) * P].bitcast(FP8X4), lhsT_scale=ls[:, s * P:(s + 1) * P],
+                    out=pn[j][:, s, :],
+                    lhsT=lq[j][:, s * P:(s + 1) * P].bitcast(FP8X4), lhsT_scale=ls[j][:, s * P:(s + 1) * P],
                     rhs=wku_q[:].bitcast(FP8X4), rhs_scale=wku_s[:], start=True, stop=True)
-            pvs = []
+            pv[j] = []
             for s in range(2):
-                pv = psum.tile([P, 512], F32, name="pv", bufs=2)
+                bank = psum.tile([P, 512], F32, name="pv", bufs=2)
                 nc.tensor.matmul_mx(
-                    out=pv[:],
-                    lhsT=lq[:, s * P:(s + 1) * P].bitcast(FP8X4), lhsT_scale=ls[:, s * P:(s + 1) * P],
+                    out=bank[:],
+                    lhsT=lq[j][:, s * P:(s + 1) * P].bitcast(FP8X4), lhsT_scale=ls[j][:, s * P:(s + 1) * P],
                     rhs=wvu_q[:].bitcast(FP8X4), rhs_scale=wvu_s[:], start=True, stop=True)
-                pvs.append(pv)
-            prods = []
+                pv[j].append(bank)
+
+        def rope_mult(j):
+            i = 2 * j % TILES
+            pd[j] = []
             for tab in (tab_c, tab_s):
-                pd = work.tile([P, 2, H, D_ROPE], F32, name="pd", bufs=4)
+                t = work.tile([P, 2, H, D_ROPE], F32, name="pd", bufs=4)
                 nc.vector.tensor_tensor(
-                    out=pd[:], in0=pr[:].rearrange("p s (h d) -> p s h d", h=H),
+                    out=t[:], in0=pr[j][:].rearrange("p s (h d) -> p s h d", h=H),
                     in1=tab[:, i:i + 2, :].unsqueeze(2).to_broadcast([P, 2, H, D_ROPE]), op=MULT)
-                prods.append(pd)
-            a = prods[0][:].rearrange("p s h (j q) -> p (s h) j q", j=2)
-            bb = prods[1][:].rearrange("p s h (j q) -> p (s h) j q", j=2)
-            kcv = kc[:].rearrange("p s h d -> p (s h) d")
-            nc.scalar.copy(out=kcv[:, :, D_ROPE:], in_=pn[:].rearrange("p s (h d) -> p (s h) d", h=H))
-            nc.vector.tensor_tensor(out=kcv[:, :, 0:D_ROPE].rearrange("p m (j q) -> p m j q", j=2), in0=a, in1=bb[:, :, ::-1, :], op=ADD)
+                pd[j].append(t)
+
+        def rope_add(j):
+            kc[j] = work.tile([P, 2 * H, HD], F32, name="kc")
+            a, b = [t[:].rearrange("p s h (j q) -> p (s h) j q", j=2) for t in pd[j]]
+            nc.vector.tensor_tensor(out=kc[j][:, :, 0:D_ROPE].rearrange("p m (j q) -> p m j q", j=2), in0=a, in1=b[:, :, ::-1, :], op=ADD)
+
+        def empty_up(j, v_engs):
+            nc.scalar.copy(out=kc[j][:, :, D_ROPE:], in_=pn[j][:].rearrange("p s (h d) -> p (s h) d", h=H))
+            vo = work.tile([P, 2, 512], F32, name="vo")
+            for s in range(2):
+                copy(v_engs[s], vo[:, s, :], pv[j][s][:])
+            b, i = divmod(2 * j, TILES)
+            nc.sync.dma_start(out=out_1.rearrange("b (p i) h d -> b p i (h d)", p=P)[b][:, i:i + 2, :], in_=vo[:])
+
+        def norm(j):
             ssq = work.tile([P, 2 * H], F32, name="ssq")
-            rinv = work.tile([P, 2 * H], F32, name="rinv")
+            rinv[j] = work.tile([P, 2 * H], F32, name="rinv")
             for m in range(2 * H):
                 junk = work.tile([P, HD], F32, name="junk", bufs=2)
-                nc.scalar.activation(out=junk[:], in_=kcv[:, m, :], func=ACT.Square, accum_out=ssq[:, m:m + 1])
-            nc.scalar.activation(out=rinv[:], in_=ssq[:], func=ACT.Abs_reciprocal_sqrt, scale=1.0 / HD, bias=EPS)
-            ko = work.tile([P, 2, H, HD], F32, name="ko")
-            kov = ko[:].rearrange("p s h d -> p (s h) d")
-            for m in range(2 * H):
-                if m % 8 in (0, 3, 6):
-                    nc.scalar.activation(out=kov[:, m, :], in_=kcv[:, m, :], func=ACT.Copy, scale=rinv[:, m:m + 1])
-                else:
-                    nc.vector.tensor_scalar(out=kov[:, m, :], in0=kcv[:, m, :], scalar1=rinv[:, m:m + 1], scalar2=None, op0=MULT)
-            for s in range(2):
-                nc.scalar.copy(out=vo[:, s, :], in_=pvs[s][:])
-            nc.sync.dma_start(out=out_1.rearrange("b (p i) h d -> b p i (h d)", p=P)[b][:, i:i + 2, :], in_=vo[:])
-            nc.sync.dma_start(out=out_0.rearrange("b (p i) h d -> b p i (h d)", p=P)[b][:, i:i + 2, :], in_=ko[:].rearrange("p s h d -> p s (h d)"))
+                nc.scalar.activation(out=junk[:], in_=kc[j][:, m, :], func=ACT.Square, accum_out=ssq[:, m:m + 1])
+            nc.scalar.activation(out=rinv[j][:], in_=ssq[:], func=ACT.Abs_reciprocal_sqrt, scale=1.0 / HD, bias=EPS)
+            ko[j] = work.tile([P, 2 * H, HD], F32, name="ko")
 
-        xb = {}
-        xq = {}
-        lq = {}
-        xb[0] = cast(0)
-        xq[0] = front(0, xb[0])
-        weight(raw_kr[0], 256, wkr_q[:, 0, :], wkr_s[:, 0, :], "kr_il0", "s")
-        weight(raw_kr[1], 256, wkr_q[:, 1, :], wkr_s[:, 1, :], "kr_il1", "v")
-        weight(raw_ku, 256, wku_q[:], wku_s[:], "ku_il", "s")
-        weight(raw_vu, 512, wvu_q[:], wvu_s[:], "vu_il", "v")
-        tab_c = keep.tile([P, TILES, D_ROPE], BF16, name="tab_c")
-        tab_s = keep.tile([P, TILES, D_ROPE], BF16, name="tab_s")
-        nc.vector.tensor_copy(out=tab_c[:, :, 0:R2], in_=cs[:])
-        nc.vector.tensor_copy(out=tab_c[:, :, R2:], in_=cs[:])
-        nc.vector.tensor_scalar(out=tab_s[:, :, 0:R2], in0=sn[:], scalar1=-1.0, scalar2=None, op0=MULT)
-        nc.vector.tensor_copy(out=tab_s[:, :, R2:], in_=sn[:])
-        for j in range(PAIRS):
-            lq[j] = latent(j, *xq[j])
-            if j + 1 < PAIRS:
-                xb[j + 1] = cast(j + 1)
-                xq[j + 1] = front(j + 1, xb[j + 1])
-            back(j, *xq[j], *lq[j])
+        def finish(j, eng, heads):
+            for m in heads:
+                if eng == "s":
+                    nc.scalar.activation(out=ko[j][:, m, :], in_=kc[j][:, m, :], func=ACT.Copy, scale=rinv[j][:, m:m + 1])
+                else:
+                    nc.vector.tensor_scalar(out=ko[j][:, m, :], in0=kc[j][:, m, :], scalar1=rinv[j][:, m:m + 1], scalar2=None, op0=MULT)
+
+        def store_k(j):
+            b, i = divmod(2 * j, TILES)
+            nc.sync.dma_start(out=out_0.rearrange("b (p i) h d -> b p i (h d)", p=P)[b][:, i:i + 2, :],
+                              in_=ko[j][:].rearrange("p (s h) d -> p s (h d)", h=H))
+
+        xb, px, xg, xq, xs, lat, lg, lq, ls, pr, pn, pv, pd, kc, rinv, ko = [{} for i in range(16)]
+        N_S = 4
+
+        with tc.manual_schedule():
+            cast(0, "vs")
+            turn(0)
+            cast(1, "gg")
+            il0 = interleave_kv(0, "s")
+            il1 = interleave_kv(1, "v")
+            scale_x(0)
+            turn(1)
+            cast(2, "gg")
+            quant(wkv_q[:, 0, :], wkv_s[:, 0, :], il0[:])
+            quant(wkv_q[:, 1, :], wkv_s[:, 1, :], il1[:])
+            kr = [interleave(raw_kr[g], 256, "kr_il%d" % g, "s") for g in range(PASSES)]
+            nc.gpsimd.tensor_copy(out=tab_c[:, :, 0:R2], in_=cs[:])
+            nc.gpsimd.tensor_copy(out=tab_c[:, :, R2:], in_=cs[:])
+            nc.gpsimd.tensor_scalar(out=tab_s[:, :, 0:R2], in0=sn[:], scalar1=-1.0, scalar2=0.0, op0=MULT, op1=ADD)
+            nc.gpsimd.tensor_copy(out=tab_s[:, :, R2:], in_=sn[:])
+            ku = interleave(raw_ku, 256, "ku_il", "g")
+            vu = interleave(raw_vu, 512, "vu_il", "s")
+            for j in range(PAIRS + 2):
+                if j < PAIRS:
+                    quant_x(j)
+                    latent(j)
+                if j == 0:
+                    for g in range(PASSES):
+                        quant(wkr_q[:, g, :], wkr_s[:, g, :], kr[g][:])
+                if j == 1:
+                    quant(wku_q[:], wku_s[:], ku[:])
+                    quant(wvu_q[:], wvu_s[:], vu[:])
+                if 0 <= j - 1 < PAIRS:
+                    quant_latent(j - 1)
+                if 0 <= j - 2:
+                    finish(j - 2, "v", range(N_S, 2 * H))
+                    store_k(j - 2)
+                if 0 <= j - 1 < PAIRS:
+                    rope_add(j - 1)
+                if j + 3 < PAIRS:
+                    if j > 0:
+                        nc.gpsimd.tensor_copy(out=token[:], in_=kc[j - 1][:, 0, 0:1])
+                    cast(j + 3, "gg")
+                if j < PAIRS:
+                    empty_latent(j)
+                if 0 <= j - 1 < PAIRS:
+                    up_mm(j - 1)
+                if j < PAIRS:
+                    rope_mm(j)
+                if j + 1 < PAIRS:
+                    scale_x(j + 1)
+                if j < PAIRS:
+                    rope_mult(j)
+                if j + 2 < PAIRS:
+                    turn(j + 2)
+                if 0 <= j - 1 < PAIRS:
+                    empty_up(j - 1, "ss")
+                    norm(j - 1)
+                    finish(j - 1, "s", range(N_S))

@@ -46,26 +46,24 @@ def tile_mlacausalselfattention_pa_t_kernel(tc, x_bytes, x_scale, cos, sin, w_kv
         load_x(0)
         sc = keep.tile([P, PASSES, 4], F32, name="sc")
         nc.scalar.dma_start(out=sc[:], in_=x_scale.rearrange("a b k -> (a b k)").rearrange("(g p t) -> p g t", p=P, t=4))
-        raw_kv = []
-        for g in range(PASSES):
-            t = stage.tile([P, 4, D_LAT], BF16, name="raw_kv%d" % g)
-            nc.sync.dma_start(out=t[:], in_=w_kv.rearrange("(g p j) c -> g p j c", p=P, j=4)[g])
-            raw_kv.append(t)
-        raw_kr = []
-        for g in range(PASSES):
-            t = stage.tile([P, 4, H * D_ROPE], BF16, name="raw_kr%d" % g)
-            nc.sync.dma_start(out=t[:], in_=w_krope.rearrange("(g p j) c -> g p j c", p=P, j=4)[g])
-            raw_kr.append(t)
         load_x(1)
-        raw_ku = stage.tile([P, 4, 256], BF16, name="raw_ku")
-        nc.sync.dma_start(out=raw_ku[:], in_=w_kup.rearrange("(p j) c -> p j c", j=4))
-        raw_vu = stage.tile([P, 4, 512], BF16, name="raw_vu")
-        nc.sync.dma_start(out=raw_vu[:], in_=w_vup.rearrange("(p j) c -> p j c", j=4))
+
+        def load_w(w, g, width, name):
+            t = stage.tile([P, 4, width], BF16, name=name)
+            nc.sync.dma_start(out=t[:], in_=w.rearrange("(g p j) c -> g p j c", p=P, j=4)[g])
+            return t
+
+        raw_kv = [load_w(w_kv, g, D_LAT, "raw_kv%d" % g) for g in range(PASSES)]
+        load_x(2)
+        raw_kr = [load_w(w_krope, g, 256, "raw_kr%d" % g) for g in range(PASSES)]
+        raw_vu = load_w(w_vup, 0, 512, "raw_vu")
+        raw_ku = load_w(w_kup, 0, 256, "raw_ku")
+        load_x(3)
         cs = stage.tile([P, TILES, R2], BF16, name="cs")
         nc.sync.dma_start(out=cs[:], in_=cos.rearrange("(p i) q -> p i q", p=P))
         sn = stage.tile([P, TILES, R2], BF16, name="sn")
         nc.sync.dma_start(out=sn[:], in_=sin.rearrange("(p i) q -> p i q", p=P))
-        for j in range(2, PAIRS):
+        for j in range(4, PAIRS):
             load_x(j)
 
         ident = keep.tile([P, P], F32, name="ident")
@@ -73,6 +71,7 @@ def tile_mlacausalselfattention_pa_t_kernel(tc, x_bytes, x_scale, cos, sin, w_kv
         warm = keep.tile([P, 1], F32, name="warm")
         warm2 = keep.tile([P, 1], F32, name="warm2")
         token = keep.tile([P, 1], F32, name="token")
+        tokenb = keep.tile([P, 1], BF16, name="tokenb")
         nc.gpsimd.memset(warm[:], 1.0)
         nc.scalar.activation(out=warm2[:], in_=warm[:], func=ACT.Abs_reciprocal_sqrt, scale=1.0 / HD, bias=EPS)
 
@@ -113,24 +112,21 @@ def tile_mlacausalselfattention_pa_t_kernel(tc, x_bytes, x_scale, cos, sin, w_kv
             for s in range(2):
                 copy(engs[s], xb[j][:, s, :], xt[j][:, s * C:(s + 1) * C].bitcast(FP8))
 
-        def turn(j):
-            px[j] = []
-            for g in range(PASSES):
-                bank = psum.tile([P, 2, 256], F32, name="px", bufs=2)
-                for s in range(2):
-                    words = xb[j][:, s, :].bitcast(F32)
-                    for u in range(2):
-                        nc.tensor.transpose(bank[:, u, s * P:(s + 1) * P], words[:, 256 * g + u:256 * (g + 1):2], ident[:])
-                px[j].append(bank)
+        def turn(j, g):
+            px[j, g] = psum.tile([P, 2, 256], F32, name="px", bufs=2)
+            for s in range(2):
+                words = xb[j][:, s, :].bitcast(F32)
+                for u in range(2):
+                    nc.tensor.transpose(px[j, g][:, u, s * P:(s + 1) * P], words[:, 256 * g + u:256 * (g + 1):2], ident[:])
 
-        def scale_x(j):
-            xg[j] = work.tile([P, PASSES, 1024], BF16, name="xg", align_bytes=64)
-            for g in range(PASSES):
-                nc.vector.tensor_tensor(
-                    out=xg[j][:, g, :].rearrange("p (n u e) -> p n u e", u=2, e=2),
-                    in0=px[j][g][:].bitcast(BF16).rearrange("p u (n e) -> p n u e", e=2),
-                    in1=sc[:, g, :].rearrange("p (u e) -> p u e", e=2).unsqueeze(1).to_broadcast([P, 256, 2, 2]),
-                    op=MULT)
+        def scale_x(j, g):
+            if g == 0:
+                xg[j] = work.tile([P, PASSES, 1024], BF16, name="xg", align_bytes=64)
+            nc.vector.tensor_tensor(
+                out=xg[j][:, g, :].rearrange("p (n u e) -> p n u e", u=2, e=2),
+                in0=px[j, g][:].bitcast(BF16).rearrange("p u (n e) -> p n u e", e=2),
+                in1=sc[:, g, :].rearrange("p (u e) -> p u e", e=2).unsqueeze(1).to_broadcast([P, 256, 2, 2]),
+                op=MULT)
 
         def quant_x(j):
             xq[j] = work.tile([P, PASSES, 256], U32, name="xq", align_bytes=64)
@@ -198,25 +194,29 @@ def tile_mlacausalselfattention_pa_t_kernel(tc, x_bytes, x_scale, cos, sin, w_kv
                 pd[j].append(t)
 
         def rope_add(j):
-            kc[j] = work.tile([P, 2 * H, HD], F32, name="kc")
+            kc[j] = work.tile([P, 2 * H, HD], F32, name="kc", bufs=5)
             a, b = [t[:].rearrange("p s h (j q) -> p (s h) j q", j=2) for t in pd[j]]
             nc.vector.tensor_tensor(out=kc[j][:, :, 0:D_ROPE].rearrange("p m (j q) -> p m j q", j=2), in0=a, in1=b[:, :, ::-1, :], op=ADD)
 
-        def empty_up(j, v_engs):
+        def empty_nope(j):
             nc.scalar.copy(out=kc[j][:, :, D_ROPE:], in_=pn[j][:].rearrange("p s (h d) -> p (s h) d", h=H))
+
+        def empty_v(j, engs):
             vo = work.tile([P, 2, 512], F32, name="vo")
             for s in range(2):
-                copy(v_engs[s], vo[:, s, :], pv[j][s][:])
+                copy(engs[s], vo[:, s, :], pv[j][s][:])
             b, i = divmod(2 * j, TILES)
             nc.sync.dma_start(out=out_1.rearrange("b (p i) h d -> b p i (h d)", p=P)[b][:, i:i + 2, :], in_=vo[:])
 
-        def norm(j):
-            ssq = work.tile([P, 2 * H], F32, name="ssq")
-            rinv[j] = work.tile([P, 2 * H], F32, name="rinv")
+        def squares(j):
+            ssq[j] = work.tile([P, 2 * H], F32, name="ssq")
             for m in range(2 * H):
                 junk = work.tile([P, HD], F32, name="junk", bufs=2)
-                nc.scalar.activation(out=junk[:], in_=kc[j][:, m, :], func=ACT.Square, accum_out=ssq[:, m:m + 1])
-            nc.scalar.activation(out=rinv[j][:], in_=ssq[:], func=ACT.Abs_reciprocal_sqrt, scale=1.0 / HD, bias=EPS)
+                nc.scalar.activation(out=junk[:], in_=kc[j][:, m, :], func=ACT.Square, accum_out=ssq[j][:, m:m + 1])
+
+        def inverse(j):
+            rinv[j] = work.tile([P, 2 * H], F32, name="rinv")
+            nc.scalar.activation(out=rinv[j][:], in_=ssq[j][:], func=ACT.Abs_reciprocal_sqrt, scale=1.0 / HD, bias=EPS)
             ko[j] = work.tile([P, 2 * H, HD], F32, name="ko")
 
         def finish(j, eng, heads):
@@ -231,61 +231,76 @@ def tile_mlacausalselfattention_pa_t_kernel(tc, x_bytes, x_scale, cos, sin, w_kv
             nc.sync.dma_start(out=out_0.rearrange("b (p i) h d -> b p i (h d)", p=P)[b][:, i:i + 2, :],
                               in_=ko[j][:].rearrange("p (s h) d -> p s (h d)", h=H))
 
-        xb, px, xg, xq, xs, lat, lg, lq, ls, pr, pn, pv, pd, kc, rinv, ko = [{} for i in range(16)]
+        xb, px, xg, xq, xs, lat, lg, lq, ls, pr, pn, pv, pd, kc, rinv, ko, ssq = [{} for i in range(17)]
         N_S = 4
+        LAST = PAIRS - 1
 
         with tc.manual_schedule():
             cast(0, "vs")
-            turn(0)
-            cast(1, "gg")
-            il0 = interleave_kv(0, "s")
-            il1 = interleave_kv(1, "v")
-            scale_x(0)
-            turn(1)
+            turn(0, 0)
+            turn(0, 1)
+            cast(1, "vv")
             cast(2, "gg")
+            il0 = interleave_kv(0, "s")
+            for g in range(PASSES):
+                scale_x(0, g)
+                turn(1, g)
+            kr = [interleave(raw_kr[g], 256, "kr_il%d" % g, "s") for g in range(PASSES)]
+            il1 = interleave_kv(1, "v")
             quant(wkv_q[:, 0, :], wkv_s[:, 0, :], il0[:])
             quant(wkv_q[:, 1, :], wkv_s[:, 1, :], il1[:])
-            kr = [interleave(raw_kr[g], 256, "kr_il%d" % g, "s") for g in range(PASSES)]
-            nc.gpsimd.tensor_copy(out=tab_c[:, :, 0:R2], in_=cs[:])
-            nc.gpsimd.tensor_copy(out=tab_c[:, :, R2:], in_=cs[:])
-            nc.gpsimd.tensor_scalar(out=tab_s[:, :, 0:R2], in0=sn[:], scalar1=-1.0, scalar2=0.0, op0=MULT, op1=ADD)
-            nc.gpsimd.tensor_copy(out=tab_s[:, :, R2:], in_=sn[:])
-            ku = interleave(raw_ku, 256, "ku_il", "g")
             vu = interleave(raw_vu, 512, "vu_il", "s")
-            for j in range(PAIRS + 2):
+            for j in range(PAIRS + 3):
                 if j < PAIRS:
                     quant_x(j)
                     latent(j)
                 if j == 0:
                     for g in range(PASSES):
                         quant(wkr_q[:, g, :], wkr_s[:, g, :], kr[g][:])
+                    nc.vector.tensor_copy(out=tab_c[:, :, 0:R2], in_=cs[:])
+                    nc.vector.tensor_copy(out=tab_c[:, :, R2:], in_=cs[:])
+                    nc.vector.tensor_scalar(out=tab_s[:, :, 0:R2], in0=sn[:], scalar1=-1.0, scalar2=None, op0=MULT)
+                    nc.vector.tensor_copy(out=tab_s[:, :, R2:], in_=sn[:])
                 if j == 1:
-                    quant(wku_q[:], wku_s[:], ku[:])
                     quant(wvu_q[:], wvu_s[:], vu[:])
+                    quant(wku_q[:], wku_s[:], ku[:])
                 if 0 <= j - 1 < PAIRS:
                     quant_latent(j - 1)
-                if 0 <= j - 2:
-                    finish(j - 2, "v", range(N_S, 2 * H))
-                    store_k(j - 2)
+                if 0 <= j - 3:
+                    finish(j - 3, "v", range(0 if j - 3 == LAST else N_S, 2 * H))
+                    store_k(j - 3)
                 if 0 <= j - 1 < PAIRS:
                     rope_add(j - 1)
                 if j + 3 < PAIRS:
                     if j > 0:
                         nc.gpsimd.tensor_copy(out=token[:], in_=kc[j - 1][:, 0, 0:1])
+                    else:
+                        nc.gpsimd.tensor_copy(out=tokenb[:], in_=tab_s[:, 0, R2:R2 + 1])
                     cast(j + 3, "gg")
                 if j < PAIRS:
                     empty_latent(j)
+                    rope_mm(j)
+                if j == 0:
+                    ku = interleave(raw_ku, 256, "ku_il", "s")
+                if j + 1 < PAIRS:
+                    scale_x(j + 1, 0)
+                if j + 2 < PAIRS:
+                    turn(j + 2, 0)
                 if 0 <= j - 1 < PAIRS:
                     up_mm(j - 1)
-                if j < PAIRS:
-                    rope_mm(j)
                 if j + 1 < PAIRS:
-                    scale_x(j + 1)
+                    scale_x(j + 1, 1)
+                if j + 2 < PAIRS:
+                    turn(j + 2, 1)
                 if j < PAIRS:
                     rope_mult(j)
-                if j + 2 < PAIRS:
-                    turn(j + 2)
+                if 0 <= j - 2 < PAIRS:
+                    squares(j - 2)
                 if 0 <= j - 1 < PAIRS:
-                    empty_up(j - 1, "ss")
-                    norm(j - 1)
-                    finish(j - 1, "s", range(N_S))
+                    empty_nope(j - 1)
+                if 0 <= j - 2 < PAIRS:
+                    inverse(j - 2)
+                if 0 <= j - 1 < PAIRS:
+                    empty_v(j - 1, "sv" if j - 1 == LAST else "ss")
+                if 0 <= j - 2 < LAST:
+                    finish(j - 2, "s", range(N_S))

@@ -47,6 +47,7 @@ def tile_mlacausalselfattention_pa_t_kernel(tc, x_bytes, x_scale, cos, sin, w_kv
         sc = keep.tile([P, PASSES, 4], F32, name="sc")
         nc.scalar.dma_start(out=sc[:], in_=x_scale.rearrange("a b k -> (a b k)").rearrange("(g p t) -> p g t", p=P, t=4))
         load_x(1)
+        load_x(2)
 
         def load_w(w, g, width, name):
             t = stage.tile([P, 4, width], BF16, name=name)
@@ -54,15 +55,14 @@ def tile_mlacausalselfattention_pa_t_kernel(tc, x_bytes, x_scale, cos, sin, w_kv
             return t
 
         raw_kv = [load_w(w_kv, g, D_LAT, "raw_kv%d" % g) for g in range(PASSES)]
-        load_x(2)
         raw_kr = [load_w(w_krope, g, 256, "raw_kr%d" % g) for g in range(PASSES)]
-        raw_vu = load_w(w_vup, 0, 512, "raw_vu")
-        raw_ku = load_w(w_kup, 0, 256, "raw_ku")
-        load_x(3)
         cs = stage.tile([P, TILES, R2], BF16, name="cs")
         nc.sync.dma_start(out=cs[:], in_=cos.rearrange("(p i) q -> p i q", p=P))
         sn = stage.tile([P, TILES, R2], BF16, name="sn")
         nc.sync.dma_start(out=sn[:], in_=sin.rearrange("(p i) q -> p i q", p=P))
+        raw_vu = load_w(w_vup, 0, 512, "raw_vu")
+        raw_ku = load_w(w_kup, 0, 256, "raw_ku")
+        load_x(3)
         for j in range(4, PAIRS):
             load_x(j)
 
@@ -71,7 +71,7 @@ def tile_mlacausalselfattention_pa_t_kernel(tc, x_bytes, x_scale, cos, sin, w_kv
         warm = keep.tile([P, 1], F32, name="warm")
         warm2 = keep.tile([P, 1], F32, name="warm2")
         token = keep.tile([P, 1], F32, name="token")
-        tokenb = keep.tile([P, 1], BF16, name="tokenb")
+        tokenb = keep.tile([P, 1], U32, name="tokenb")
         nc.gpsimd.memset(warm[:], 1.0)
         nc.scalar.activation(out=warm2[:], in_=warm[:], func=ACT.Abs_reciprocal_sqrt, scale=1.0 / HD, bias=EPS)
 
@@ -104,13 +104,15 @@ def tile_mlacausalselfattention_pa_t_kernel(tc, x_bytes, x_scale, cos, sin, w_kv
 
         def interleave(raw, width, name, eng):
             t = stage.tile([P, width * 4], BF16, name=name, align_bytes=64)
-            copy(eng, t[:].rearrange("p (c j) -> p c j", j=4), raw[:].rearrange("p j c -> p c j"))
+            copy(eng, t[:].rearrange("p (c i j) -> p c j i", i=4, j=4), raw[:].rearrange("p j (c i) -> p c j i", i=4))
             return t
 
         def cast(j, engs):
             xb[j] = work.tile([P, 2, C], BF16, name="xb", bufs=3)
-            for s in range(2):
-                copy(engs[s], xb[j][:, s, :], xt[j][:, s * C:(s + 1) * C].bitcast(FP8))
+            n = 2 * C // len(engs)
+            flat = xb[j][:].rearrange("p s k -> p (s k)")
+            for q, eng in enumerate(engs):
+                copy(eng, flat[:, q * n:(q + 1) * n], xt[j][:, q * n:(q + 1) * n].bitcast(FP8))
 
         def turn(j, g):
             px[j, g] = psum.tile([P, 2, 256], F32, name="px", bufs=2)
@@ -183,124 +185,186 @@ def tile_mlacausalselfattention_pa_t_kernel(tc, x_bytes, x_scale, cos, sin, w_kv
                     rhs=wvu_q[:].bitcast(FP8X4), rhs_scale=wvu_s[:], start=True, stop=True)
                 pv[j].append(bank)
 
-        def rope_mult(j):
+        def rope_mult(j, which):
             i = 2 * j % TILES
-            pd[j] = []
-            for tab in (tab_c, tab_s):
-                t = work.tile([P, 2, H, D_ROPE], F32, name="pd", bufs=4)
-                nc.vector.tensor_tensor(
-                    out=t[:], in0=pr[j][:].rearrange("p s (h d) -> p s h d", h=H),
-                    in1=tab[:, i:i + 2, :].unsqueeze(2).to_broadcast([P, 2, H, D_ROPE]), op=MULT)
-                pd[j].append(t)
+            tab = (tab_c, tab_s)[which]
+            t = work.tile([P, 2, H, D_ROPE], F32, name="pd", bufs=4)
+            nc.vector.tensor_tensor(
+                out=t[:], in0=pr[j][:].rearrange("p s (h d) -> p s h d", h=H),
+                in1=tab[:, i:i + 2, :].unsqueeze(2).to_broadcast([P, 2, H, D_ROPE]), op=MULT)
+            pd[j, which] = t
 
         def rope_add(j):
             kc[j] = work.tile([P, 2 * H, HD], F32, name="kc", bufs=5)
-            a, b = [t[:].rearrange("p s h (j q) -> p (s h) j q", j=2) for t in pd[j]]
+            a, b = [t[:].rearrange("p s h (j q) -> p (s h) j q", j=2) for t in (pd[j, 0], pd[j, 1])]
             nc.vector.tensor_tensor(out=kc[j][:, :, 0:D_ROPE].rearrange("p m (j q) -> p m j q", j=2), in0=a, in1=b[:, :, ::-1, :], op=ADD)
 
         def empty_nope(j):
             nc.scalar.copy(out=kc[j][:, :, D_ROPE:], in_=pn[j][:].rearrange("p s (h d) -> p (s h) d", h=H))
 
-        def empty_v(j, engs):
-            vo = work.tile([P, 2, 512], F32, name="vo")
-            for s in range(2):
-                copy(engs[s], vo[:, s, :], pv[j][s][:])
-            b, i = divmod(2 * j, TILES)
-            nc.sync.dma_start(out=out_1.rearrange("b (p i) h d -> b p i (h d)", p=P)[b][:, i:i + 2, :], in_=vo[:])
+        def empty_v(j, s, eng):
+            if s == 0:
+                vo[j] = work.tile([P, 2, 512], F32, name="vo")
+            copy(eng, vo[j][:, s, :], pv[j][s][:])
 
-        def squares(j):
-            ssq[j] = work.tile([P, 2 * H], F32, name="ssq")
-            for m in range(2 * H):
-                junk = work.tile([P, HD], F32, name="junk", bufs=2)
-                nc.scalar.activation(out=junk[:], in_=kc[j][:, m, :], func=ACT.Square, accum_out=ssq[j][:, m:m + 1])
+        def store_v(j):
+            b, i = divmod(2 * j, TILES)
+            nc.sync.dma_start(out=out_1.rearrange("b (p i) h d -> b p i (h d)", p=P)[b][:, i:i + 2, :], in_=vo[j][:])
+
+        def squares(j, eng, heads):
+            if j not in ssq:
+                ssq[j] = work.tile([P, 2 * H], F32, name="ssq")
+            for m in heads:
+                if eng == "s":
+                    junk = work.tile([P, HD], F32, name="junk", bufs=2)
+                    nc.scalar.activation(out=junk[:], in_=kc[j][:, m, :], func=ACT.Square, accum_out=ssq[j][:, m:m + 1])
+                else:
+                    junkv = work.tile([P, HD], F32, name="junkv", bufs=2)
+                    nc.vector.scalar_tensor_tensor(out=junkv[:], in0=kc[j][:, m, :], scalar=1.0, in1=kc[j][:, m, :], op0=MULT, op1=MULT, accum_out=ssq[j][:, m:m + 1])
 
         def inverse(j):
             rinv[j] = work.tile([P, 2 * H], F32, name="rinv")
             nc.scalar.activation(out=rinv[j][:], in_=ssq[j][:], func=ACT.Abs_reciprocal_sqrt, scale=1.0 / HD, bias=EPS)
-            ko[j] = work.tile([P, 2 * H, HD], F32, name="ko")
+            ko[j] = work.tile([P, 2 * H, HD], F32, name="ko", bufs=4)
 
         def finish(j, eng, heads):
             for m in heads:
                 if eng == "s":
                     nc.scalar.activation(out=ko[j][:, m, :], in_=kc[j][:, m, :], func=ACT.Copy, scale=rinv[j][:, m:m + 1])
-                else:
+                elif eng == "v":
                     nc.vector.tensor_scalar(out=ko[j][:, m, :], in0=kc[j][:, m, :], scalar1=rinv[j][:, m:m + 1], scalar2=None, op0=MULT)
+                else:
+                    nc.gpsimd.tensor_scalar(out=ko[j][:, m, :], in0=kc[j][:, m, :], scalar1=rinv[j][:, m:m + 1], scalar2=0.0, op0=MULT, op1=ADD)
 
-        def store_k(j):
+        def store_k(j, lo=0, hi=2):
             b, i = divmod(2 * j, TILES)
-            nc.sync.dma_start(out=out_0.rearrange("b (p i) h d -> b p i (h d)", p=P)[b][:, i:i + 2, :],
-                              in_=ko[j][:].rearrange("p (s h) d -> p s (h d)", h=H))
+            nc.sync.dma_start(out=out_0.rearrange("b (p i) h d -> b p i (h d)", p=P)[b][:, i + lo:i + hi, :],
+                              in_=ko[j][:, lo * H:hi * H, :].rearrange("p (s h) d -> p s (h d)", h=H))
 
-        xb, px, xg, xq, xs, lat, lg, lq, ls, pr, pn, pv, pd, kc, rinv, ko, ssq = [{} for i in range(17)]
-        N_S = 4
+        xb, px, xg, xq, xs, lat, lg, lq, ls, pr, pn, pv, pd, kc, rinv, ko, ssq, vo = [{} for i in range(18)]
         LAST = PAIRS - 1
+
+        def split(j):
+            if j >= LAST - 2:
+                a, b = 0, 0
+            elif j >= LAST - 5:
+                a, b = 6, 2
+            else:
+                a, b = 2, 4
+            return list(range(0, a)), list(range(a, a + b)), list(range(a + b, 2 * H))
 
         with tc.manual_schedule():
             cast(0, "vs")
             turn(0, 0)
             turn(0, 1)
             cast(1, "vv")
-            cast(2, "gg")
+            cast(2, "g")
             il0 = interleave_kv(0, "s")
-            for g in range(PASSES):
-                scale_x(0, g)
-                turn(1, g)
+            scale_x(0, 0)
+            turn(1, 0)
+            scale_x(0, 1)
+            turn(1, 1)
             kr = [interleave(raw_kr[g], 256, "kr_il%d" % g, "s") for g in range(PASSES)]
             il1 = interleave_kv(1, "v")
             quant(wkv_q[:, 0, :], wkv_s[:, 0, :], il0[:])
             quant(wkv_q[:, 1, :], wkv_s[:, 1, :], il1[:])
-            vu = interleave(raw_vu, 512, "vu_il", "s")
-            for j in range(PAIRS + 3):
-                if j < PAIRS:
-                    quant_x(j)
-                    latent(j)
+            nc.scalar.copy(out=tab_c[:, :, 0:R2], in_=cs[:])
+            nc.scalar.copy(out=tab_c[:, :, R2:], in_=cs[:])
+            nc.scalar.activation(out=tab_s[:, :, 0:R2], in_=sn[:], func=ACT.Copy, scale=-1.0)
+            nc.scalar.copy(out=tab_s[:, :, R2:], in_=sn[:])
+            for j in range(LAST):
+                quant_x(j)
+                latent(j)
                 if j == 0:
                     for g in range(PASSES):
                         quant(wkr_q[:, g, :], wkr_s[:, g, :], kr[g][:])
-                    nc.vector.tensor_copy(out=tab_c[:, :, 0:R2], in_=cs[:])
-                    nc.vector.tensor_copy(out=tab_c[:, :, R2:], in_=cs[:])
-                    nc.vector.tensor_scalar(out=tab_s[:, :, 0:R2], in0=sn[:], scalar1=-1.0, scalar2=None, op0=MULT)
-                    nc.vector.tensor_copy(out=tab_s[:, :, R2:], in_=sn[:])
+
+                if j >= 1:
+                    quant_latent(j - 1)
+                if j >= 3:
+                    finish(j - 3, "v", split(j - 3)[2])
+                if j >= 1:
+                    rope_add(j - 1)
                 if j == 1:
+                    ku = interleave(raw_ku, 256, "ku_il", "v")
                     quant(wvu_q[:], wvu_s[:], vu[:])
                     quant(wku_q[:], wku_s[:], ku[:])
-                if 0 <= j - 1 < PAIRS:
-                    quant_latent(j - 1)
-                if 0 <= j - 3:
-                    finish(j - 3, "v", range(0 if j - 3 == LAST else N_S, 2 * H))
-                    store_k(j - 3)
-                if 0 <= j - 1 < PAIRS:
-                    rope_add(j - 1)
+                if j >= 1:
+                    nc.gpsimd.tensor_copy(out=token[:], in_=kc[j - 1][:, 0, 0:1])
+                else:
+                    nc.gpsimd.tensor_copy(out=tokenb[:], in_=wkr_q[:, 1, 0:1])
                 if j + 3 < PAIRS:
-                    if j > 0:
-                        nc.gpsimd.tensor_copy(out=token[:], in_=kc[j - 1][:, 0, 0:1])
-                    else:
-                        nc.gpsimd.tensor_copy(out=tokenb[:], in_=tab_s[:, 0, R2:R2 + 1])
-                    cast(j + 3, "gg")
-                if j < PAIRS:
-                    empty_latent(j)
-                    rope_mm(j)
+                    cast(j + 3, "g")
+                if j >= 3:
+                    finish(j - 3, "g", split(j - 3)[0])
+                    store_k(j - 3)
+                empty_latent(j)
+                rope_mm(j)
                 if j == 0:
-                    ku = interleave(raw_ku, 256, "ku_il", "s")
-                if j + 1 < PAIRS:
-                    scale_x(j + 1, 0)
+                    vu = interleave(raw_vu, 512, "vu_il", "s")
+                scale_x(j + 1, 0)
                 if j + 2 < PAIRS:
                     turn(j + 2, 0)
-                if 0 <= j - 1 < PAIRS:
+                if j >= 1:
                     up_mm(j - 1)
-                if j + 1 < PAIRS:
-                    scale_x(j + 1, 1)
+                scale_x(j + 1, 1)
                 if j + 2 < PAIRS:
                     turn(j + 2, 1)
-                if j < PAIRS:
-                    rope_mult(j)
-                if 0 <= j - 2 < PAIRS:
-                    squares(j - 2)
-                if 0 <= j - 1 < PAIRS:
+                rope_mult(j, 0)
+                if j == LAST - 1:
+                    quant_x(LAST)
+                rope_mult(j, 1)
+                if j >= 2:
+                    squares(j - 2, "s", range(2 * H))
+                if j >= 1:
                     empty_nope(j - 1)
-                if 0 <= j - 2 < PAIRS:
+                if j >= 2:
                     inverse(j - 2)
-                if 0 <= j - 1 < PAIRS:
-                    empty_v(j - 1, "sv" if j - 1 == LAST else "ss")
-                if 0 <= j - 2 < LAST:
-                    finish(j - 2, "s", range(N_S))
+                if j >= 1:
+                    empty_v(j - 1, 0, "s")
+                    empty_v(j - 1, 1, "s")
+                    store_v(j - 1)
+                if j >= 2:
+                    finish(j - 2, "s", split(j - 2)[1])
+
+            latent(LAST)
+            quant_latent(LAST - 1)
+            rope_add(LAST - 1)
+            nc.gpsimd.tensor_copy(out=token[:], in_=kc[LAST - 1][:, 0, 0:1])
+            finish(LAST - 3, "g", split(LAST - 3)[0])
+            finish(LAST - 3, "v", split(LAST - 3)[2])
+            store_k(LAST - 3)
+            up_mm(LAST - 1)
+            empty_latent(LAST)
+            rope_mm(LAST)
+            squares(LAST - 2, "s", range(0, 5))
+            squares(LAST - 2, "v", range(5, 2 * H))
+            empty_v(LAST - 1, 0, "v")
+            empty_v(LAST - 1, 1, "v")
+            store_v(LAST - 1)
+            rope_mult(LAST, 0)
+            quant_latent(LAST)
+            up_mm(LAST)
+            rope_mult(LAST, 1)
+            empty_nope(LAST - 1)
+            inverse(LAST - 2)
+            squares(LAST - 1, "s", range(0, 4))
+            finish(LAST - 2, "v", range(2 * H))
+            store_k(LAST - 2)
+            rope_add(LAST)
+            squares(LAST - 1, "v", range(4, 2 * H))
+            empty_nope(LAST)
+            inverse(LAST - 1)
+            empty_v(LAST, 0, "s")
+            empty_v(LAST, 1, "v")
+            store_v(LAST)
+            squares(LAST, "s", range(0, 5))
+            squares(LAST, "v", range(5, 2 * H))
+            finish(LAST - 1, "v", range(2 * H))
+            store_k(LAST - 1)
+            inverse(LAST)
+            finish(LAST, "v", range(0, 4))
+            finish(LAST, "s", range(5, 8))
+            store_k(LAST, 0, 1)
+            finish(LAST, "v", range(4, 5))
+            store_k(LAST, 1, 2)

from contextlib import ExitStack

import concourse.mybir as mybir
from concourse.masks import make_identity

F32 = mybir.dt.float32
BF16 = mybir.dt.bfloat16
U32 = mybir.dt.uint32
U8 = mybir.dt.uint8
FP8 = mybir.dt.float8_e4m3fn
FP8X4 = mybir.dt.float8_e4m3fn_x4
ADD = mybir.AluOpType.add
MULT = mybir.AluOpType.mult
ACT = mybir.ActivationFunctionType

P = 128
B, T, C = 2, 2048, 1024
D_LAT = 512
H, HD, D_ROPE = 4, 128, 64
R2 = D_ROPE // 2
PASSES = C // 512
TILES = T // P
PAIRS = B * TILES // 2
EPS = 1.1920928955078125e-07

FLOPS = 2 * B * T * (C * D_LAT + D_LAT * H * (HD - D_ROPE) + D_LAT * H * HD + C * H * D_ROPE)


def tile_mlacausalselfattention_pa_t_kernel(tc, x_bytes, x_scale, cos, sin, w_kv, w_kup, w_vup, w_krope, out_0, out_1):
    nc = tc.nc
    with ExitStack() as ctx:
        keep = ctx.enter_context(tc.tile_pool(name="keep", bufs=1))
        stage = ctx.enter_context(tc.tile_pool(name="stage", bufs=1))
        work = ctx.enter_context(tc.tile_pool(name="work", bufs=3))
        psum = ctx.enter_context(tc.psum_pool(name="psum", bufs=1))

        x_view = x_bytes.rearrange("b (p i) k -> b p (i k)", p=P)
        xt = []
        for j in range(PAIRS):
            xt.append(keep.tile([P, 2 * C], U8, name="xbytes%d" % j))

        def load_x(j):
            b, i = divmod(2 * j, TILES)
            nc.sync.dma_start(out=xt[j][:], in_=x_view[b][:, i * C:(i + 2) * C])

        load_x(0)
        sc = keep.tile([P, PASSES, 4], F32, name="sc")
        nc.scalar.dma_start(out=sc[:], in_=x_scale.rearrange("a b k -> (a b k)").rearrange("(g p t) -> p g t", p=P, t=4))
        load_x(1)
        load_x(2)

        def load_w(w, g, width, name):
            t = stage.tile([P, 4, width], BF16, name=name)
            nc.sync.dma_start(out=t[:], in_=w.rearrange("(g p j) c -> g p j c", p=P, j=4)[g])
            return t

        raw_kv = [load_w(w_kv, g, D_LAT, "raw_kv%d" % g) for g in range(PASSES)]
        raw_kr = [load_w(w_krope, g, 256, "raw_kr%d" % g) for g in range(PASSES)]
        cs = stage.tile([P, TILES, R2], BF16, name="cs")
        nc.sync.dma_start(out=cs[:], in_=cos.rearrange("(p i) q -> p i q", p=P))
        sn = stage.tile([P, TILES, R2], BF16, name="sn")
        nc.sync.dma_start(out=sn[:], in_=sin.rearrange("(p i) q -> p i q", p=P))
        raw_vu = load_w(w_vup, 0, 512, "raw_vu")
        raw_ku = load_w(w_kup, 0, 256, "raw_ku")
        load_x(3)
        for j in range(4, PAIRS):
            load_x(j)

        ident = keep.tile([P, P], F32, name="ident")
        make_identity(nc, ident[:])
        warm = keep.tile([P, 1], F32, name="warm")
        warm2 = keep.tile([P, 1], F32, name="warm2")
        token = keep.tile([P, 1], F32, name="token")
        tokenb = keep.tile([P, 1], U32, name="tokenb")
        nc.gpsimd.memset(warm[:], 1.0)
        nc.scalar.activation(out=warm2[:], in_=warm[:], func=ACT.Abs_reciprocal_sqrt, scale=1.0 / HD, bias=EPS)

        wkv_q = keep.tile([P, PASSES, D_LAT], U32, name="wkv_q", align_bytes=64)
        wkv_s = keep.tile([P, PASSES, D_LAT], U8, name="wkv_s", align_bytes=64)
        wkr_q = keep.tile([P, PASSES, 256], U32, name="wkr_q", align_bytes=64)
        wkr_s = keep.tile([P, PASSES, 256], U8, name="wkr_s", align_bytes=64)
        wku_q = keep.tile([P, 256], U32, name="wku_q", align_bytes=64)
        wku_s = keep.tile([P, 256], U8, name="wku_s", align_bytes=64)
        wvu_q = keep.tile([P, 512], U32, name="wvu_q", align_bytes=64)
        wvu_s = keep.tile([P, 512], U8, name="wvu_s", align_bytes=64)
        tab_c = keep.tile([P, TILES, D_ROPE], BF16, name="tab_c")
        tab_s = keep.tile([P, TILES, D_ROPE], BF16, name="tab_s")

        def quant(codes, scales, src):
            nc.vector.quantize_mx(out=codes.bitcast(FP8X4), scales=scales, in_=src)

        def copy(eng, dst, src):
            if eng == "s":
                nc.scalar.copy(out=dst, in_=src)
            elif eng == "v":
                nc.vector.tensor_copy(out=dst, in_=src)
            else:
                nc.gpsimd.tensor_copy(out=dst, in_=src)

        def interleave_kv(g, eng):
            t = stage.tile([P, 4 * D_LAT], BF16, name="kv_il%d" % g, align_bytes=64)
            copy(eng, t[:].rearrange("p (t m j) -> p t m j", t=4, j=4), raw_kv[g][:].rearrange("p j (m t) -> p t m j", t=4))
            return t

        def interleave(raw, width, name, eng):
            t = stage.tile([P, width * 4], BF16, name=name, align_bytes=64)
            copy(eng, t[:].rearrange("p (c i j) -> p c j i", i=4, j=4), raw[:].rearrange("p j (c i) -> p c j i", i=4))
            return t

        def cast(j, engs):
            xb[j] = work.tile([P, 2, C], BF16, name="xb", bufs=3)
            n = 2 * C // len(engs)
            flat = xb[j][:].rearrange("p s k -> p (s k)")
            for q, eng in enumerate(engs):
                copy(eng, flat[:, q * n:(q + 1) * n], xt[j][:, q * n:(q + 1) * n].bitcast(FP8))

        def turn(j, g):
            px[j, g] = psum.tile([P, 2, 256], F32, name="px", bufs=2)
            for s in range(2):
                words = xb[j][:, s, :].bitcast(F32)
                for u in range(2):
                    nc.tensor.transpose(px[j, g][:, u, s * P:(s + 1) * P], words[:, 256 * g + u:256 * (g + 1):2], ident[:])

        def scale_x(j, g):
            if g == 0:
                xg[j] = work.tile([P, PASSES, 1024], BF16, name="xg", align_bytes=64)
            nc.vector.tensor_tensor(
                out=xg[j][:, g, :].rearrange("p (n u e) -> p n u e", u=2, e=2),
                in0=px[j, g][:].bitcast(BF16).rearrange("p u (n e) -> p n u e", e=2),
                in1=sc[:, g, :].rearrange("p (u e) -> p u e", e=2).unsqueeze(1).to_broadcast([P, 256, 2, 2]),
                op=MULT)

        def quant_x(j):
            xq[j] = work.tile([P, PASSES, 256], U32, name="xq", align_bytes=64)
            xs[j] = work.tile([P, PASSES, 256], U8, name="xs", align_bytes=64)
            for g in range(PASSES):
                quant(xq[j][:, g, :], xs[j][:, g, :], xg[j][:, g, :])

        def latent(j):
            lat[j] = []
            for s in range(2):
                bank = psum.tile([P, 4, P], F32, name="lat", bufs=2)
                for t in range(4):
                    for g in range(PASSES):
                        nc.tensor.matmul_mx(
                            out=bank[:, t, :],
                            lhsT=wkv_q[:, g, t * P:(t + 1) * P].bitcast(FP8X4), lhsT_scale=wkv_s[:, g, t * P:(t + 1) * P],
                            rhs=xq[j][:, g, s * P:(s + 1) * P].bitcast(FP8X4), rhs_scale=xs[j][:, g, s * P:(s + 1) * P],
                            start=(g == 0), stop=(g == PASSES - 1))
                lat[j].append(bank)

        def empty_latent(j):
            lg[j] = work.tile([P, 2, 512], BF16, name="lg", align_bytes=64)
            for s in range(2):
                nc.scalar.copy(out=lg[j][:, s, :].rearrange("p (n t) -> p n t", t=4), in_=lat[j][s][:].rearrange("p t n -> p n t"))

        def quant_latent(j):
            lq[j] = work.tile([P, 256], U32, name="lq", align_bytes=64)
            ls[j] = work.tile([P, 256], U8, name="ls", align_bytes=64)
            quant(lq[j][:], ls[j][:], lg[j][:].rearrange("p s w -> p (s w)"))

        def rope_mm(j):
            pr[j] = psum.tile([P, 2, 256], F32, name="pr")
            for s in range(2):
                for g in range(PASSES):
                    nc.tensor.matmul_mx(
                        out=pr[j][:, s, :],
                        lhsT=xq[j][:, g, s * P:(s + 1) * P].bitcast(FP8X4), lhsT_scale=xs[j][:, g, s * P:(s + 1) * P],
                        rhs=wkr_q[:, g, :].bitcast(FP8X4), rhs_scale=wkr_s[:, g, :],
                        start=(g == 0), stop=(g == PASSES - 1))

        def up_mm(j):
            pn[j] = psum.tile([P, 2, 256], F32, name="pn")
            for s in range(2):
                nc.tensor.matmul_mx(
                    out=pn[j][:, s, :],
                    lhsT=lq[j][:, s * P:(s + 1) * P].bitcast(FP8X4), lhsT_scale=ls[j][:, s * P:(s + 1) * P],
                    rhs=wku_q[:].bitcast(FP8X4), rhs_scale=wku_s[:], start=True, stop=True)
            pv[j] = []
            for s in range(2):
                bank = psum.tile([P, 512], F32, name="pv", bufs=2)
                nc.tensor.matmul_mx(
                    out=bank[:],
                    lhsT=lq[j][:, s * P:(s + 1) * P].bitcast(FP8X4), lhsT_scale=ls[j][:, s * P:(s + 1) * P],
                    rhs=wvu_q[:].bitcast(FP8X4), rhs_scale=wvu_s[:], start=True, stop=True)
                pv[j].append(bank)

        def rope_mult(j, which):
            i = 2 * j % TILES
            tab = (tab_c, tab_s)[which]
            t = work.tile([P, 2, H, D_ROPE], F32, name="pd", bufs=4)
            nc.vector.tensor_tensor(
                out=t[:], in0=pr[j][:].rearrange("p s (h d) -> p s h d", h=H),
                in1=tab[:, i:i + 2, :].unsqueeze(2).to_broadcast([P, 2, H, D_ROPE]), op=MULT)
            pd[j, which] = t

        def rope_add(j):
            kc[j] = work.tile([P, 2 * H, HD], F32, name="kc", bufs=5)
            a, b = [t[:].rearrange("p s h (j q) -> p (s h) j q", j=2) for t in (pd[j, 0], pd[j, 1])]
            nc.vector.tensor_tensor(out=kc[j][:, :, 0:D_ROPE].rearrange("p m (j q) -> p m j q", j=2), in0=a, in1=b[:, :, ::-1, :], op=ADD)

        def empty_nope(j):
            nc.scalar.copy(out=kc[j][:, :, D_ROPE:], in_=pn[j][:].rearrange("p s (h d) -> p (s h) d", h=H))

        def empty_v(j, s, eng):
            if s == 0:
                vo[j] = work.tile([P, 2, 512], F32, name="vo")
            copy(eng, vo[j][:, s, :], pv[j][s][:])

        def store_v(j):
            b, i = divmod(2 * j, TILES)
            nc.sync.dma_start(out=out_1.rearrange("b (p i) h d -> b p i (h d)", p=P)[b][:, i:i + 2, :], in_=vo[j][:])

        def squares(j, eng, heads):
            if j not in ssq:
                ssq[j] = work.tile([P, 2 * H], F32, name="ssq")
            for m in heads:
                if eng == "s":
                    junk = work.tile([P, HD], F32, name="junk", bufs=2)
                    nc.scalar.activation(out=junk[:], in_=kc[j][:, m, :], func=ACT.Square, accum_out=ssq[j][:, m:m + 1])
                else:
                    junkv = work.tile([P, HD], F32, name="junkv", bufs=2)
                    nc.vector.scalar_tensor_tensor(out=junkv[:], in0=kc[j][:, m, :], scalar=1.0, in1=kc[j][:, m, :], op0=MULT, op1=MULT, accum_out=ssq[j][:, m:m + 1])

        def inverse(j):
            rinv[j] = work.tile([P, 2 * H], F32, name="rinv")
            nc.scalar.activation(out=rinv[j][:], in_=ssq[j][:], func=ACT.Abs_reciprocal_sqrt, scale=1.0 / HD, bias=EPS)
            ko[j] = work.tile([P, 2 * H, HD], F32, name="ko", bufs=4)

        def finish(j, eng, heads):
            for m in heads:
                if eng == "s":
                    nc.scalar.activation(out=ko[j][:, m, :], in_=kc[j][:, m, :], func=ACT.Copy, scale=rinv[j][:, m:m + 1])
                elif eng == "v":
                    nc.vector.tensor_scalar(out=ko[j][:, m, :], in0=kc[j][:, m, :], scalar1=rinv[j][:, m:m + 1], scalar2=None, op0=MULT)
                else:
                    nc.gpsimd.tensor_scalar(out=ko[j][:, m, :], in0=kc[j][:, m, :], scalar1=rinv[j][:, m:m + 1], scalar2=0.0, op0=MULT, op1=ADD)

        def store_k(j, lo=0, hi=2):
            b, i = divmod(2 * j, TILES)
            nc.sync.dma_start(out=out_0.rearrange("b (p i) h d -> b p i (h d)", p=P)[b][:, i + lo:i + hi, :],
                              in_=ko[j][:, lo * H:hi * H, :].rearrange("p (s h) d -> p s (h d)", h=H))

        xb, px, xg, xq, xs, lat, lg, lq, ls, pr, pn, pv, pd, kc, rinv, ko, ssq, vo = [{} for i in range(18)]
        LAST = PAIRS - 1

        def split(j):
            if j >= LAST - 2:
                a, b = 0, 0
            elif j >= LAST - 5:
                a, b = 6, 2
            else:
                a, b = 2, 4
            return list(range(0, a)), list(range(a, a + b)), list(range(a + b, 2 * H))

        with tc.manual_schedule():
            cast(0, "vs")
            turn(0, 0)
            turn(0, 1)
            cast(1, "vv")
            cast(2, "g")
            il0 = interleave_kv(0, "s")
            scale_x(0, 0)
            turn(1, 0)
            scale_x(0, 1)
            turn(1, 1)
            kr = [interleave(raw_kr[g], 256, "kr_il%d" % g, "s") for g in range(PASSES)]
            il1 = interleave_kv(1, "v")
            quant(wkv_q[:, 0, :], wkv_s[:, 0, :], il0[:])
            quant(wkv_q[:, 1, :], wkv_s[:, 1, :], il1[:])
            nc.scalar.copy(out=tab_c[:, :, 0:R2], in_=cs[:])
            nc.scalar.copy(out=tab_c[:, :, R2:], in_=cs[:])
            nc.scalar.activation(out=tab_s[:, :, 0:R2], in_=sn[:], func=ACT.Copy, scale=-1.0)
            nc.scalar.copy(out=tab_s[:, :, R2:], in_=sn[:])
            for j in range(LAST):
                quant_x(j)
                latent(j)
                if j == 0:
                    for g in range(PASSES):
                        quant(wkr_q[:, g, :], wkr_s[:, g, :], kr[g][:])

                if j >= 1:
                    quant_latent(j - 1)
                if j >= 3:
                    finish(j - 3, "v", split(j - 3)[2])
                if j >= 1:
                    rope_add(j - 1)
                if j == 1:
                    ku = interleave(raw_ku, 256, "ku_il", "v")
                    quant(wvu_q[:], wvu_s[:], vu[:])
                    quant(wku_q[:], wku_s[:], ku[:])
                if j >= 1:
                    nc.gpsimd.tensor_copy(out=token[:], in_=kc[j - 1][:, 0, 0:1])
                else:
                    nc.gpsimd.tensor_copy(out=tokenb[:], in_=wkr_q[:, 1, 0:1])
                if j + 3 < PAIRS:
                    cast(j + 3, "g")
                if j >= 3:
                    finish(j - 3, "g", split(j - 3)[0])
                    store_k(j - 3)
                empty_latent(j)
                rope_mm(j)
                if j == 0:
                    vu = interleave(raw_vu, 512, "vu_il", "s")
                scale_x(j + 1, 0)
                if j + 2 < PAIRS:
                    turn(j + 2, 0)
                if j >= 1:
                    up_mm(j - 1)
                scale_x(j + 1, 1)
                if j + 2 < PAIRS:
                    turn(j + 2, 1)
                rope_mult(j, 0)
                if j == LAST - 1:
                    quant_x(LAST)
                rope_mult(j, 1)
                if j >= 2:
                    squares(j - 2, "s", range(2 * H))
                if j >= 1:
                    empty_nope(j - 1)
                if j >= 2:
                    inverse(j - 2)
                if j >= 1:
                    empty_v(j - 1, 0, "s")
                    empty_v(j - 1, 1, "s")
                    store_v(j - 1)
                if j >= 2:
                    finish(j - 2, "s", split(j - 2)[1])

            latent(LAST)
            quant_latent(LAST - 1)
            rope_add(LAST - 1)
            nc.gpsimd.tensor_copy(out=token[:], in_=kc[LAST - 1][:, 0, 0:1])
            finish(LAST - 3, "g", split(LAST - 3)[0])
            finish(LAST - 3, "v", split(LAST - 3)[2])
            store_k(LAST - 3)
            up_mm(LAST - 1)
            empty_latent(LAST)
            rope_mm(LAST)
            squares(LAST - 2, "s", range(0, 5))
            squares(LAST - 2, "v", range(5, 2 * H))
            empty_v(LAST - 1, 0, "v")
            empty_v(LAST - 1, 1, "v")
            store_v(LAST - 1)
            rope_mult(LAST, 0)
            quant_latent(LAST)
            up_mm(LAST)
            rope_mult(LAST, 1)
            empty_nope(LAST - 1)
            inverse(LAST - 2)
            squares(LAST - 1, "s", range(0, 4))
            finish(LAST - 2, "v", range(2 * H))
            store_k(LAST - 2)
            rope_add(LAST)
            squares(LAST - 1, "v", range(4, 2 * H))
            empty_nope(LAST)
            inverse(LAST - 1)
            empty_v(LAST, 0, "s")
            empty_v(LAST, 1, "v")
            store_v(LAST)
            squares(LAST, "s", range(0, 5))
            squares(LAST, "v", range(5, 2 * H))
            finish(LAST - 1, "v", range(2 * H))
            store_k(LAST - 1)
            inverse(LAST)
            finish(LAST, "v", range(0, 4))
            finish(LAST, "s", range(5, 8))
            store_k(LAST, 0, 1)
            finish(LAST, "v", range(4, 5))
            store_k(LAST, 1, 2)
